import numpy as np
import ml_dtypes


def mxq(x, axis, fmt="e4m3"):
    dtype, down = {"e4m3": (ml_dtypes.float8_e4m3fn, 7), "e5m2": (ml_dtypes.float8_e5m2, 14)}[fmt]
    v = np.moveaxis(np.asarray(x, np.float32).astype(ml_dtypes.bfloat16).astype(np.float64), axis, -1)
    blocks = v.reshape(v.shape[:-1] + (-1, 32))
    amax = np.abs(blocks).max(-1, keepdims=True)
    byte = np.maximum(np.where(amax > 0, np.frexp(amax)[1] - 1 + 127, 0) - down, 1)
    scale = np.exp2(byte - 127.0)
    codes = (blocks / scale).astype(np.float32).astype(dtype).astype(np.float64)
    return np.moveaxis((codes * scale).reshape(v.shape), -1, axis)


WIDE = False


def mx_kscale(k):
    if not WIDE:
        return np.ones(k)
    levels = np.array([10, -10, 5, -5, 0])
    a = np.random.permutation(np.resize(levels, k // 512 * 4)).reshape(k // 512, 4)
    idx = np.arange(k)
    return np.exp2(a[idx // 512, idx % 128 // 32])


BF16 = ml_dtypes.bfloat16


def bf(x):
    return np.asarray(x, np.float32).astype(BF16)


def f64(x):
    return np.asarray(x).astype(np.float64)


B, T, D, H, HD, F = 2, 512, 1024, 16, 64, 4096
A = H * HD
EPS = 1e-5
ERF_H = 0.5
ERF_N = 14


def layernorm(x, g, b):
    mu = np.mean(x, axis=-1, keepdims=True)
    var = np.mean(np.square(x - mu), axis=-1, keepdims=True)
    return (x - mu) / np.sqrt(var + EPS) * g + b


def erf(z):
    acc = np.zeros_like(z)
    for n in range(ERF_N):
        tn = (n + 0.5) * ERF_H
        acc = acc + np.exp(-tn * tn) / (tn * tn + z * z)
    return np.tanh(np.pi * z / ERF_H) - 2.0 * ERF_H * z * np.exp(-z * z) / np.pi * acc


def gelu_erf(v):
    return 0.5 * v * (1.0 + erf(v / np.sqrt(2.0)))


def setup_inputs():
    s, t = mx_kscale(A), mx_kscale(D)
    return {"attn": bf(np.random.standard_normal((B, T, A)) * 0.25 * s),
            "x": bf(np.random.standard_normal((B, T, D)) + 0.5 * np.random.standard_normal((B, T, 1))),
            "w_out": bf(np.random.standard_normal((A, D)) * 2.0 / np.sqrt(A) / s[:, None]),
            "b_out": bf(0.1 * np.random.standard_normal(D)),
            "ln2_g": bf((1.0 + 0.1 * np.random.standard_normal(D)) * t),
            "ln2_b": bf(0.1 * np.random.standard_normal(D) * t),
            "w1": bf(np.random.standard_normal((D, F)) / np.sqrt(D) / t[:, None]),
            "b1": bf(0.2 * np.random.standard_normal(F))}


def reference(attn, x, w_out, b_out, ln2_g, ln2_b, w1, b1):
    x_mid = f64(x) + ((mxq(f64(attn), 2, "e4m3") @ mxq(f64(w_out), 0, "e4m3")) + f64(b_out))
    h2 = layernorm(x_mid, f64(ln2_g), f64(ln2_b))
    hid = gelu_erf((mxq(h2, 2, "e4m3") @ mxq(f64(w1), 0, "e4m3")) + f64(b1))
    return x_mid, hid

@@ -1,0 +1,276 @@
+from contextlib import ExitStack
+
+import concourse.masks as masks
+import concourse.mybir as mybir
+
+F32 = mybir.dt.float32
+BF16 = mybir.dt.bfloat16
+U32 = mybir.dt.uint32
+U8 = mybir.dt.uint8
+FP8X4 = mybir.dt.float8_e4m3fn_x4
+ALU = mybir.AluOpType
+ACT = mybir.ActivationFunctionType
+
+P = 128
+PACK = 4
+K_PASS = P * PACK
+BANK = 512
+RUN = 4
+
+TOKENS = 1024
+WIDTH = 1024
+HIDDEN = 4096
+EPS = 1e-5
+TOKEN_TILES = TOKENS // P
+K_ROWS = WIDTH // P
+PASSES = WIDTH // K_PASS
+CHUNK = 1024
+CHUNKS = HIDDEN // CHUNK
+PIECE = BANK
+PIECES_PER_CHUNK = PASSES * (CHUNK // PIECE)
+W1_PIECES = CHUNKS * PIECES_PER_CHUNK
+EARLY_PIECES = TOKEN_TILES
+
+FLOPS = 2 * TOKENS * WIDTH * WIDTH + 2 * TOKENS * WIDTH * HIDDEN
+
+
+def regroup(copy, grouped, rows):
+    copy(
+        out=grouped.rearrange("p (a i t) -> p a t i", i=RUN, t=PACK),
+        in_=rows.rearrange("p t (a i) -> p a t i", i=RUN),
+    )
+
+
+def tile_transformerblock_pb_kernel(tc, attn, x, w_out, b_out, ln2_g, ln2_b, w1, b1, out_0, out_1):
+    nc = tc.nc
+    attn_rows = attn.flatten_outer_dims().rearrange("(p i) k -> p i k", i=TOKEN_TILES)
+    x_rows = x.flatten_outer_dims().rearrange("(p i) d -> p i d", i=TOKEN_TILES)
+    x_mid_rows = out_0.flatten_outer_dims().rearrange("(p i) d -> p i d", i=TOKEN_TILES)
+    hid_rows = out_1.flatten_outer_dims().rearrange("(p i) f -> p i f", i=TOKEN_TILES)
+    w_out_rows = w_out.rearrange("(g u q e) n -> g q u e n", g=PASSES, u=2, q=P, e=2)
+    w1_rows = w1.rearrange("(c t p) f -> p (c t) f", c=PASSES, t=PACK, p=P)
+
+    with ExitStack() as ctx:
+        keep = ctx.enter_context(tc.tile_pool(name="keep", bufs=1))
+        raw = ctx.enter_context(tc.tile_pool(name="raw", bufs=4))
+        pieces = ctx.enter_context(tc.tile_pool(name="pieces", bufs=3))
+        packs = ctx.enter_context(tc.tile_pool(name="packs", bufs=2))
+        rows = ctx.enter_context(tc.tile_pool(name="rows", bufs=2))
+        stats = ctx.enter_context(tc.tile_pool(name="stats", bufs=3))
+        results = ctx.enter_context(tc.tile_pool(name="results", bufs=4))
+        psum = ctx.enter_context(tc.psum_pool(name="psum", bufs=8))
+
+        def bank(name):
+            return psum.tile([P, BANK], F32, name=name, tag="bank")
+
+        b_out_all = keep.tile([P, WIDTH], BF16, name="b_out_all")
+        nc.scalar.dma_start(out=b_out_all[:], in_=b_out.partition_broadcast(P))
+        gain_bias_rows = keep.tile([P, P], BF16, name="gain_bias_rows")
+        nc.vector.memset(gain_bias_rows[:], 0.0)
+        nc.scalar.dma_start(out=gain_bias_rows[0:K_ROWS, :], in_=ln2_g.rearrange("(r p) -> r p", p=P))
+        nc.scalar.dma_start(out=gain_bias_rows[K_ROWS : 2 * K_ROWS, :], in_=ln2_b.rearrange("(r p) -> r p", p=P))
+
+        def raw_tile(name):
+            return raw.tile([P, PASSES * PACK, CHUNK], BF16, name=name, tag="raw")
+
+        w_out_raw = raw_tile("w_out_raw")
+        for g in range(PASSES):
+            nc.sync.dma_start(
+                out=w_out_raw[:, PACK * g : PACK * (g + 1), :].rearrange("q (u e) n -> q u e n", u=2),
+                in_=w_out_rows[g],
+            )
+        attn_raw = raw_tile("attn_raw")
+        half = TOKEN_TILES // 2
+        for h in range(2):
+            nc.sync.dma_start(out=attn_raw[:, half * h : half * (h + 1), :], in_=attn_rows[:, half * h : half * (h + 1), :])
+        x_raw = keep.tile([P, TOKEN_TILES, WIDTH], BF16, name="x_raw")
+        nc.sync.dma_start(out=x_raw[:], in_=x_rows)
+        w1_raw = []
+        for j in range(CHUNKS):
+            w1_raw.append(raw_tile("w1_raw%d" % j))
+            nc.sync.dma_start(out=w1_raw[j][:], in_=w1_rows[:, :, CHUNK * j : CHUNK * (j + 1)])
+        b1_all = keep.tile([P, HIDDEN], BF16, name="b1_all")
+        nc.sync.dma_start(out=b1_all[:], in_=b1.partition_broadcast(P))
+
+        neg_half = keep.tile([P, 1], F32, name="neg_half")
+        nc.vector.memset(neg_half[:], -0.5)
+        table_warm = keep.tile([P, 1], F32, name="table_warm")
+        nc.scalar.activation(out=table_warm[:], in_=neg_half[:], func=ACT.Gelu)
+        identity = keep.tile([P, P], F32, name="identity")
+        masks.make_identity(nc, identity[:])
+
+        def quantised(name, outer, width):
+            words = keep.tile([P, outer, width], U32, name=name + "_words", align_bytes=64)
+            scales = keep.tile([P, outer, width], U8, name=name + "_scales", align_bytes=64)
+            return words, scales
+
+        w_out_words, w_out_scales = quantised("w_out", PASSES, WIDTH)
+        w1_words, w1_scales = quantised("w1", PASSES, HIDDEN)
+        attn_words, attn_scales = quantised("attn", TOKEN_TILES, PASSES * P)
+        h2_words, h2_scales = quantised("h2", TOKEN_TILES, PASSES * P)
+
+        def quantise(grouped, words, scales):
+            nc.vector.quantize_mx(out=words.bitcast(FP8X4), scales=scales, in_=grouped)
+
+        def multiply(acc, lhs_words, lhs_scales, i, rhs_words, rhs_scales, cols):
+            for c in range(PASSES):
+                tokens = slice(P * c, P * (c + 1))
+                nc.tensor.matmul_mx(
+                    out=acc,
+                    lhsT=lhs_words[:, i, tokens].bitcast(FP8X4),
+                    lhsT_scale=lhs_scales[:, i, tokens],
+                    rhs=rhs_words[:, c, cols].bitcast(FP8X4),
+                    rhs_scale=rhs_scales[:, c, cols],
+                    start=(c == 0),
+                    stop=(c == PASSES - 1),
+                )
+
+        piece_tiles = {}
+
+        def regroup_piece(key, copy, raw_rows):
+            piece_tiles[key] = pieces.tile([P, PACK * PIECE], BF16, name="piece", tag="piece", align_bytes=64)
+            regroup(copy, piece_tiles[key][:], raw_rows)
+
+        def w1_piece(k):
+            j, rest = divmod(k, PIECES_PER_CHUNK)
+            c, n = divmod(rest, CHUNK // PIECE)
+            return j, c, slice(CHUNK * j + PIECE * n, CHUNK * j + PIECE * (n + 1)), slice(PIECE * n, PIECE * (n + 1))
+
+        def regroup_w1_piece(k, copy):
+            j, c, cols, cols_in_chunk = w1_piece(k)
+            regroup_piece(("w1", k), copy, w1_raw[j][:, PACK * c : PACK * (c + 1), cols_in_chunk])
+
+        def quantise_w1_piece(k):
+            j, c, cols, cols_in_chunk = w1_piece(k)
+            quantise(piece_tiles[("w1", k)][:], w1_words[:, c, cols], w1_scales[:, c, cols])
+
+        w_out_pieces = [(g, slice(PIECE * n, PIECE * (n + 1))) for g in range(PASSES) for n in range(WIDTH // PIECE)]
+        for k in range(len(w_out_pieces) + 1):
+            if k < len(w_out_pieces):
+                g, cols = w_out_pieces[k]
+                copy = nc.vector.tensor_copy if k % 2 == 0 else nc.scalar.copy
+                regroup_piece(("w_out", k), copy, w_out_raw[:, PACK * g : PACK * (g + 1), cols])
+            if k > 0:
+                g, cols = w_out_pieces[k - 1]
+                quantise(piece_tiles[("w_out", k - 1)][:], w_out_words[:, g, cols], w_out_scales[:, g, cols])
+
+        for i in range(TOKEN_TILES):
+            attn_pairs = attn_raw[:, i, :].bitcast(F32)
+            attn_t = bank("attn_t")
+            for g in range(PASSES):
+                for u in range(2):
+                    block = 2 * g + u
+                    nc.tensor.transpose(
+                        out=attn_t[:, PASSES * P * u + P * g : PASSES * P * u + P * (g + 1)],
+                        in_=attn_pairs[:, P * block : P * (block + 1)],
+                        identity=identity[:],
+                    )
+            attn_grouped = packs.tile([P, PACK * PASSES * P], BF16, name="attn_grouped", align_bytes=64)
+            nc.scalar.copy(
+                out=attn_grouped[:].bitcast(F32).rearrange("q (m u) -> q m u", u=2),
+                in_=attn_t[:].rearrange("q (u m) -> q m u", u=2),
+            )
+            quantise(attn_grouped[:], attn_words[:, i, :], attn_scales[:, i, :])
+
+        gain_bias_f32 = keep.tile([P, P], F32, name="gain_bias_f32")
+        nc.vector.tensor_copy(out=gain_bias_f32[:], in_=gain_bias_rows[:])
+        gain_bias_t = bank("gain_bias_t")
+        nc.tensor.transpose(out=gain_bias_t[:, 0:P], in_=gain_bias_f32[:], identity=identity[:])
+        gain_bias = keep.tile([P, 2 * K_ROWS], F32, name="gain_bias")
+        nc.vector.tensor_copy(out=gain_bias[:], in_=gain_bias_t[:, 0 : 2 * K_ROWS])
+
+        x_mid = {}
+        neg_mean = {}
+        rstd = {}
+        normed = {}
+        h2_planes = {}
+        h2_grouped = {}
+
+        def project(i):
+            x_bias = rows.tile([P, WIDTH], F32, name="x_bias")
+            nc.vector.tensor_tensor(out=x_bias[:], in0=x_raw[:, i, :], in1=b_out_all[:], op=ALU.add)
+            x_mid[i] = rows.tile([P, WIDTH], F32, name="x_mid", bufs=3)
+            row_sums = stats.tile([P, WIDTH // BANK], F32, name="row_sums")
+            for n in range(WIDTH // BANK):
+                cols = slice(BANK * n, BANK * (n + 1))
+                acc = bank("acc1")
+                multiply(acc[:], attn_words, attn_scales, i, w_out_words, w_out_scales, cols)
+                nc.vector.scalar_tensor_tensor(
+                    out=x_mid[i][:, cols], in0=acc[:], scalar=1.0, in1=x_bias[:, cols],
+                    op0=ALU.mult, op1=ALU.add, accum_out=row_sums[:, n : n + 1],
+                )
+            nc.sync.dma_start(out=x_mid_rows[:, i, :], in_=x_mid[i][:])
+            scaled_sums = stats.tile([P, WIDTH // BANK], F32, name="scaled_sums")
+            neg_mean[i] = stats.tile([P, 1], F32, name="neg_mean")
+            nc.scalar.activation(
+                out=scaled_sums[:], in_=row_sums[:], func=ACT.Identity, scale=-1.0 / WIDTH, accum_out=neg_mean[i][:]
+            )
+            normed[i] = rows.tile([P, WIDTH], F32, name="normed")
+            sum_sq = stats.tile([P, 1], F32, name="sum_sq")
+            nc.scalar.activation(
+                out=normed[i][:], in_=x_mid[i][:], func=ACT.Square, bias=neg_mean[i][:], accum_out=sum_sq[:]
+            )
+            var_eps = stats.tile([P, 1], F32, name="var_eps")
+            nc.gpsimd.tensor_scalar(
+                out=var_eps[:], in0=sum_sq[:], scalar1=1.0 / WIDTH, scalar2=EPS, op0=ALU.mult, op1=ALU.add
+            )
+            rstd[i] = stats.tile([P, 1], F32, name="rstd")
+            nc.gpsimd.tensor_tensor(out=rstd[i][:], in0=var_eps[:], in1=neg_half[:], op=ALU.pow)
+
+        def normalise_and_transpose(i):
+            nc.vector.tensor_scalar(
+                out=normed[i][:], in0=x_mid[i][:], scalar1=neg_mean[i][:], scalar2=rstd[i][:],
+                op0=ALU.add, op1=ALU.mult,
+            )
+            h2_planes[i] = packs.tile([P, PACK, PASSES * P], BF16, name="h2_planes")
+            for c in range(PASSES):
+                normed_t = bank("normed_t")
+                for t in range(PACK):
+                    r = PACK * c + t
+                    nc.tensor.transpose(
+                        out=normed_t[:, P * t : P * (t + 1)], in_=normed[i][:, P * r : P * (r + 1)], identity=identity[:]
+                    )
+                for t in range(PACK):
+                    r = PACK * c + t
+                    nc.scalar.activation(
+                        out=h2_planes[i][:, t, P * c : P * (c + 1)], in_=normed_t[:, P * t : P * (t + 1)],
+                        func=ACT.Identity, scale=gain_bias[:, r : r + 1], bias=gain_bias[:, K_ROWS + r : K_ROWS + r + 1],
+                    )
+
+        def regroup_h2(i):
+            h2_grouped[i] = packs.tile([P, PACK * PASSES * P], BF16, name="h2_grouped", align_bytes=64)
+            regroup(nc.vector.tensor_copy, h2_grouped[i][:], h2_planes[i][:])
+
+        def quantise_h2(i):
+            quantise(h2_grouped[i][:], h2_words[:, i, :], h2_scales[:, i, :])
+
+        for s in range(TOKEN_TILES + 2):
+            if s >= 2:
+                regroup_h2(s - 2)
+            if s < TOKEN_TILES:
+                project(s)
+            if s >= 2:
+                quantise_h2(s - 2)
+            if 1 <= s <= TOKEN_TILES:
+                normalise_and_transpose(s - 1)
+                quantise_w1_piece(s - 1)
+            if s < EARLY_PIECES:
+                regroup_w1_piece(s, nc.scalar.copy)
+
+        for j in range(CHUNKS):
+            for i in range(TOKEN_TILES):
+                late, odd = divmod(TOKEN_TILES * j + i, 2)
+                k = EARLY_PIECES + late
+                prepare = odd == 0 and k < W1_PIECES
+                if prepare:
+                    regroup_w1_piece(k, nc.vector.tensor_copy)
+                hid = results.tile([P, CHUNK], F32, name="hid")
+                for n in range(CHUNK // BANK):
+                    cols = slice(CHUNK * j + BANK * n, CHUNK * j + BANK * (n + 1))
+                    acc = bank("acc2")
+                    multiply(acc[:], h2_words, h2_scales, i, w1_words, w1_scales, cols)
+                    nc.vector.tensor_tensor(out=hid[:, BANK * n : BANK * (n + 1)], in0=acc[:], in1=b1_all[:, cols], op=ALU.add)
+                if prepare:
+                    quantise_w1_piece(k)
+                nc.scalar.activation(out=hid[:], in_=hid[:], func=ACT.Gelu)
+                nc.sync.dma_start(out=hid_rows[:, i, CHUNK * j : CHUNK * (j + 1)], in_=hid[:])

@@ -29,7 +29,9 @@ CHUNKS = HIDDEN // CHUNK
 PIECE = BANK
 PIECES_PER_CHUNK = PASSES * (CHUNK // PIECE)
 W1_PIECES = CHUNKS * PIECES_PER_CHUNK
-EARLY_PIECES = TOKEN_TILES
+FIRST_TILES = 2
+DRAIN = 2
+ROUNDS = TOKEN_TILES + DRAIN
 
 FLOPS = 2 * TOKENS * WIDTH * WIDTH + 2 * TOKENS * WIDTH * HIDDEN
 
@@ -52,13 +54,14 @@ def tile_transformerblock_pb_kernel(tc, attn, x, w_out, b_out, ln2_g, ln2_b, w1,
 
     with ExitStack() as ctx:
         keep = ctx.enter_context(tc.tile_pool(name="keep", bufs=1))
-        raw = ctx.enter_context(tc.tile_pool(name="raw", bufs=4))
+        raw = ctx.enter_context(tc.tile_pool(name="raw", bufs=3))
         pieces = ctx.enter_context(tc.tile_pool(name="pieces", bufs=3))
         packs = ctx.enter_context(tc.tile_pool(name="packs", bufs=2))
         rows = ctx.enter_context(tc.tile_pool(name="rows", bufs=2))
         stats = ctx.enter_context(tc.tile_pool(name="stats", bufs=3))
-        results = ctx.enter_context(tc.tile_pool(name="results", bufs=4))
+        results = ctx.enter_context(tc.tile_pool(name="results", bufs=8))
         psum = ctx.enter_context(tc.psum_pool(name="psum", bufs=8))
+        ctx.enter_context(tc.manual_schedule())
 
         def bank(name):
             return psum.tile([P, BANK], F32, name=name, tag="bank")
@@ -73,6 +76,10 @@ def tile_transformerblock_pb_kernel(tc, attn, x, w_out, b_out, ln2_g, ln2_b, w1,
         def raw_tile(name):
             return raw.tile([P, PASSES * PACK, CHUNK], BF16, name=name, tag="raw")
 
+        def load_w1_chunk(j):
+            w1_raw[j] = raw_tile("w1_raw%d" % j)
+            nc.sync.dma_start(out=w1_raw[j][:], in_=w1_rows[:, :, CHUNK * j : CHUNK * (j + 1)])
+
         w_out_raw = raw_tile("w_out_raw")
         for g in range(PASSES):
             nc.sync.dma_start(
@@ -80,15 +87,13 @@ def tile_transformerblock_pb_kernel(tc, attn, x, w_out, b_out, ln2_g, ln2_b, w1,
                 in_=w_out_rows[g],
             )
         attn_raw = raw_tile("attn_raw")
-        half = TOKEN_TILES // 2
-        for h in range(2):
-            nc.sync.dma_start(out=attn_raw[:, half * h : half * (h + 1), :], in_=attn_rows[:, half * h : half * (h + 1), :])
         x_raw = keep.tile([P, TOKEN_TILES, WIDTH], BF16, name="x_raw")
-        nc.sync.dma_start(out=x_raw[:], in_=x_rows)
-        w1_raw = []
-        for j in range(CHUNKS):
-            w1_raw.append(raw_tile("w1_raw%d" % j))
-            nc.sync.dma_start(out=w1_raw[j][:], in_=w1_rows[:, :, CHUNK * j : CHUNK * (j + 1)])
+        for tiles in (slice(0, FIRST_TILES), slice(FIRST_TILES, TOKEN_TILES)):
+            nc.sync.dma_start(out=attn_raw[:, tiles, :], in_=attn_rows[:, tiles, :])
+            nc.sync.dma_start(out=x_raw[:, tiles, :], in_=x_rows[:, tiles, :])
+        w1_raw = {}
+        for j in range(CHUNKS - 1):
+            load_w1_chunk(j)
         b1_all = keep.tile([P, HIDDEN], BF16, name="b1_all")
         nc.sync.dma_start(out=b1_all[:], in_=b1.partition_broadcast(P))
 
@@ -143,6 +148,15 @@ def tile_transformerblock_pb_kernel(tc, attn, x, w_out, b_out, ln2_g, ln2_b, w1,
         def quantise_w1_piece(k):
             j, c, cols, cols_in_chunk = w1_piece(k)
             quantise(piece_tiles[("w1", k)][:], w1_words[:, c, cols], w1_scales[:, c, cols])
+
+        def prepare_w1(slot):
+            k, odd_slot = divmod(slot, 2)
+            if odd_slot:
+                return
+            if k < W1_PIECES:
+                regroup_w1_piece(k, nc.vector.tensor_copy if k % 2 == 0 else nc.scalar.copy)
+            if 1 <= k <= W1_PIECES:
+                quantise_w1_piece(k - 1)
 
         w_out_pieces = [(g, slice(PIECE * n, PIECE * (n + 1))) for g in range(PASSES) for n in range(WIDTH // PIECE)]
         for k in range(len(w_out_pieces) + 1):
@@ -244,33 +258,27 @@ def tile_transformerblock_pb_kernel(tc, attn, x, w_out, b_out, ln2_g, ln2_b, w1,
         def quantise_h2(i):
             quantise(h2_grouped[i][:], h2_words[:, i, :], h2_scales[:, i, :])
 
-        for s in range(TOKEN_TILES + 2):
-            if s >= 2:
-                regroup_h2(s - 2)
+        for s in range(ROUNDS):
             if s < TOKEN_TILES:
                 project(s)
-            if s >= 2:
-                quantise_h2(s - 2)
             if 1 <= s <= TOKEN_TILES:
                 normalise_and_transpose(s - 1)
-                quantise_w1_piece(s - 1)
-            if s < EARLY_PIECES:
-                regroup_w1_piece(s, nc.scalar.copy)
+            if s >= 2:
+                regroup_h2(s - 2)
+            prepare_w1(s)
+            if s >= 2:
+                quantise_h2(s - 2)
+            if s == TOKEN_TILES - 1:
+                load_w1_chunk(CHUNKS - 1)
 
         for j in range(CHUNKS):
             for i in range(TOKEN_TILES):
-                late, odd = divmod(TOKEN_TILES * j + i, 2)
-                k = EARLY_PIECES + late
-                prepare = odd == 0 and k < W1_PIECES
-                if prepare:
-                    regroup_w1_piece(k, nc.vector.tensor_copy)
                 hid = results.tile([P, CHUNK], F32, name="hid")
                 for n in range(CHUNK // BANK):
                     cols = slice(CHUNK * j + BANK * n, CHUNK * j + BANK * (n + 1))
                     acc = bank("acc2")
                     multiply(acc[:], h2_words, h2_scales, i, w1_words, w1_scales, cols)
                     nc.vector.tensor_tensor(out=hid[:, BANK * n : BANK * (n + 1)], in0=acc[:], in1=b1_all[:, cols], op=ALU.add)
-                if prepare:
-                    quantise_w1_piece(k)
+                prepare_w1(ROUNDS + TOKEN_TILES * j + i)
                 nc.scalar.activation(out=hid[:], in_=hid[:], func=ACT.Gelu)
                 nc.sync.dma_start(out=hid_rows[:, i, CHUNK * j : CHUNK * (j + 1)], in_=hid[:])

@@ -61,17 +61,16 @@ def tile_transformerblock_pb_kernel(tc, attn, x, w_out, b_out, ln2_g, ln2_b, w1,
         stats = ctx.enter_context(tc.tile_pool(name="stats", bufs=3))
         results = ctx.enter_context(tc.tile_pool(name="results", bufs=8))
         psum = ctx.enter_context(tc.psum_pool(name="psum", bufs=8))
-        ctx.enter_context(tc.manual_schedule())
 
         def bank(name):
             return psum.tile([P, BANK], F32, name=name, tag="bank")
 
         b_out_all = keep.tile([P, WIDTH], BF16, name="b_out_all")
-        nc.scalar.dma_start(out=b_out_all[:], in_=b_out.partition_broadcast(P))
+        nc.sync.dma_start(out=b_out_all[:], in_=b_out.partition_broadcast(P))
         gain_bias_rows = keep.tile([P, P], BF16, name="gain_bias_rows")
         nc.vector.memset(gain_bias_rows[:], 0.0)
-        nc.scalar.dma_start(out=gain_bias_rows[0:K_ROWS, :], in_=ln2_g.rearrange("(r p) -> r p", p=P))
-        nc.scalar.dma_start(out=gain_bias_rows[K_ROWS : 2 * K_ROWS, :], in_=ln2_b.rearrange("(r p) -> r p", p=P))
+        nc.sync.dma_start(out=gain_bias_rows[0:K_ROWS, :], in_=ln2_g.rearrange("(r p) -> r p", p=P))
+        nc.sync.dma_start(out=gain_bias_rows[K_ROWS : 2 * K_ROWS, :], in_=ln2_b.rearrange("(r p) -> r p", p=P))
 
         def raw_tile(name):
             return raw.tile([P, PASSES * PACK, CHUNK], BF16, name=name, tag="raw")
@@ -202,7 +201,7 @@ def tile_transformerblock_pb_kernel(tc, attn, x, w_out, b_out, ln2_g, ln2_b, w1,
 
         def project(i):
             x_bias = rows.tile([P, WIDTH], F32, name="x_bias")
-            nc.vector.tensor_tensor(out=x_bias[:], in0=x_raw[:, i, :], in1=b_out_all[:], op=ALU.add)
+            nc.gpsimd.tensor_tensor(out=x_bias[:], in0=x_raw[:, i, :], in1=b_out_all[:], op=ALU.add)
             x_mid[i] = rows.tile([P, WIDTH], F32, name="x_mid", bufs=3)
             row_sums = stats.tile([P, WIDTH // BANK], F32, name="row_sums")
             for n in range(WIDTH // BANK):

@@ -201,7 +201,7 @@ def tile_transformerblock_pb_kernel(tc, attn, x, w_out, b_out, ln2_g, ln2_b, w1,
 
         def project(i):
             x_bias = rows.tile([P, WIDTH], F32, name="x_bias")
-            nc.gpsimd.tensor_tensor(out=x_bias[:], in0=x_raw[:, i, :], in1=b_out_all[:], op=ALU.add)
+            nc.vector.tensor_tensor(out=x_bias[:], in0=x_raw[:, i, :], in1=b_out_all[:], op=ALU.add)
             x_mid[i] = rows.tile([P, WIDTH], F32, name="x_mid", bufs=3)
             row_sums = stats.tile([P, WIDTH // BANK], F32, name="row_sums")
             for n in range(WIDTH // BANK):

@@ -29,9 +29,9 @@ CHUNKS = HIDDEN // CHUNK
 PIECE = BANK
 PIECES_PER_CHUNK = PASSES * (CHUNK // PIECE)
 W1_PIECES = CHUNKS * PIECES_PER_CHUNK
+VECTOR_EVERY = 4
+FILL = 2
 FIRST_TILES = 2
-DRAIN = 2
-ROUNDS = TOKEN_TILES + DRAIN
 
 FLOPS = 2 * TOKENS * WIDTH * WIDTH + 2 * TOKENS * WIDTH * HIDDEN
 
@@ -57,9 +57,7 @@ def tile_transformerblock_pb_kernel(tc, attn, x, w_out, b_out, ln2_g, ln2_b, w1,
         raw = ctx.enter_context(tc.tile_pool(name="raw", bufs=3))
         pieces = ctx.enter_context(tc.tile_pool(name="pieces", bufs=3))
         packs = ctx.enter_context(tc.tile_pool(name="packs", bufs=2))
-        rows = ctx.enter_context(tc.tile_pool(name="rows", bufs=2))
-        stats = ctx.enter_context(tc.tile_pool(name="stats", bufs=3))
-        results = ctx.enter_context(tc.tile_pool(name="results", bufs=8))
+        rows = ctx.enter_context(tc.tile_pool(name="rows", bufs=14))
         psum = ctx.enter_context(tc.psum_pool(name="psum", bufs=8))
 
         def bank(name):
@@ -96,10 +94,10 @@ def tile_transformerblock_pb_kernel(tc, attn, x, w_out, b_out, ln2_g, ln2_b, w1,
         b1_all = keep.tile([P, HIDDEN], BF16, name="b1_all")
         nc.sync.dma_start(out=b1_all[:], in_=b1.partition_broadcast(P))
 
-        neg_half = keep.tile([P, 1], F32, name="neg_half")
+        neg_half = keep.tile([P, TOKEN_TILES], F32, name="neg_half")
         nc.vector.memset(neg_half[:], -0.5)
         table_warm = keep.tile([P, 1], F32, name="table_warm")
-        nc.scalar.activation(out=table_warm[:], in_=neg_half[:], func=ACT.Gelu)
+        nc.scalar.activation(out=table_warm[:], in_=neg_half[:, 0:1], func=ACT.Gelu)
         identity = keep.tile([P, P], F32, name="identity")
         masks.make_identity(nc, identity[:])
 
@@ -148,12 +146,9 @@ def tile_transformerblock_pb_kernel(tc, attn, x, w_out, b_out, ln2_g, ln2_b, w1,
             j, c, cols, cols_in_chunk = w1_piece(k)
             quantise(piece_tiles[("w1", k)][:], w1_words[:, c, cols], w1_scales[:, c, cols])
 
-        def prepare_w1(slot):
-            k, odd_slot = divmod(slot, 2)
-            if odd_slot:
-                return
+        def prepare_w1(k):
             if k < W1_PIECES:
-                regroup_w1_piece(k, nc.vector.tensor_copy if k % 2 == 0 else nc.scalar.copy)
+                regroup_w1_piece(k, nc.vector.tensor_copy if k % VECTOR_EVERY == 0 else nc.scalar.copy)
             if 1 <= k <= W1_PIECES:
                 quantise_w1_piece(k - 1)
 
@@ -167,7 +162,9 @@ def tile_transformerblock_pb_kernel(tc, attn, x, w_out, b_out, ln2_g, ln2_b, w1,
                 g, cols = w_out_pieces[k - 1]
                 quantise(piece_tiles[("w_out", k - 1)][:], w_out_words[:, g, cols], w_out_scales[:, g, cols])
 
-        for i in range(TOKEN_TILES):
+        attn_grouped = {}
+
+        def transpose_attn(i):
             attn_pairs = attn_raw[:, i, :].bitcast(F32)
             attn_t = bank("attn_t")
             for g in range(PASSES):
@@ -178,12 +175,19 @@ def tile_transformerblock_pb_kernel(tc, attn, x, w_out, b_out, ln2_g, ln2_b, w1,
                         in_=attn_pairs[:, P * block : P * (block + 1)],
                         identity=identity[:],
                     )
-            attn_grouped = packs.tile([P, PACK * PASSES * P], BF16, name="attn_grouped", align_bytes=64)
+            attn_grouped[i] = packs.tile([P, PACK * PASSES * P], BF16, name="attn_grouped", align_bytes=64)
             nc.scalar.copy(
-                out=attn_grouped[:].bitcast(F32).rearrange("q (m u) -> q m u", u=2),
+                out=attn_grouped[i][:].bitcast(F32).rearrange("q (m u) -> q m u", u=2),
                 in_=attn_t[:].rearrange("q (u m) -> q m u", u=2),
             )
-            quantise(attn_grouped[:], attn_words[:, i, :], attn_scales[:, i, :])
+
+        def quantise_attn(i):
+            quantise(attn_grouped[i][:], attn_words[:, i, :], attn_scales[:, i, :])
+
+        for i in range(FIRST_TILES):
+            transpose_attn(i)
+        for i in range(FIRST_TILES):
+            quantise_attn(i)
 
         gain_bias_f32 = keep.tile([P, P], F32, name="gain_bias_f32")
         nc.vector.tensor_copy(out=gain_bias_f32[:], in_=gain_bias_rows[:])
@@ -192,63 +196,80 @@ def tile_transformerblock_pb_kernel(tc, attn, x, w_out, b_out, ln2_g, ln2_b, w1,
         gain_bias = keep.tile([P, 2 * K_ROWS], F32, name="gain_bias")
         nc.vector.tensor_copy(out=gain_bias[:], in_=gain_bias_t[:, 0 : 2 * K_ROWS])
 
+        def row(name):
+            return rows.tile([P, WIDTH], F32, name=name, tag="row")
+
         x_mid = {}
-        neg_mean = {}
-        rstd = {}
-        normed = {}
-        h2_planes = {}
-        h2_grouped = {}
+        row_sums = keep.tile([P, TOKEN_TILES, WIDTH // BANK], F32, name="row_sums")
+        scaled_sums = keep.tile([P, WIDTH // BANK], F32, name="scaled_sums")
+        neg_mean = keep.tile([P, TOKEN_TILES], F32, name="neg_mean")
+        squares = keep.tile([P, WIDTH], BF16, name="squares")
+        sum_sq = keep.tile([P, TOKEN_TILES], F32, name="sum_sq")
 
         def project(i):
-            x_bias = rows.tile([P, WIDTH], F32, name="x_bias")
+            x_bias = row("x_bias")
             nc.vector.tensor_tensor(out=x_bias[:], in0=x_raw[:, i, :], in1=b_out_all[:], op=ALU.add)
-            x_mid[i] = rows.tile([P, WIDTH], F32, name="x_mid", bufs=3)
-            row_sums = stats.tile([P, WIDTH // BANK], F32, name="row_sums")
+            x_mid[i] = row("x_mid")
             for n in range(WIDTH // BANK):
                 cols = slice(BANK * n, BANK * (n + 1))
                 acc = bank("acc1")
                 multiply(acc[:], attn_words, attn_scales, i, w_out_words, w_out_scales, cols)
                 nc.vector.scalar_tensor_tensor(
                     out=x_mid[i][:, cols], in0=acc[:], scalar=1.0, in1=x_bias[:, cols],
-                    op0=ALU.mult, op1=ALU.add, accum_out=row_sums[:, n : n + 1],
+                    op0=ALU.mult, op1=ALU.add, accum_out=row_sums[:, i, n : n + 1],
                 )
             nc.sync.dma_start(out=x_mid_rows[:, i, :], in_=x_mid[i][:])
-            scaled_sums = stats.tile([P, WIDTH // BANK], F32, name="scaled_sums")
-            neg_mean[i] = stats.tile([P, 1], F32, name="neg_mean")
             nc.scalar.activation(
-                out=scaled_sums[:], in_=row_sums[:], func=ACT.Identity, scale=-1.0 / WIDTH, accum_out=neg_mean[i][:]
+                out=scaled_sums[:], in_=row_sums[:, i, :], func=ACT.Identity, scale=-1.0 / WIDTH,
+                accum_out=neg_mean[:, i : i + 1],
             )
-            normed[i] = rows.tile([P, WIDTH], F32, name="normed")
-            sum_sq = stats.tile([P, 1], F32, name="sum_sq")
             nc.scalar.activation(
-                out=normed[i][:], in_=x_mid[i][:], func=ACT.Square, bias=neg_mean[i][:], accum_out=sum_sq[:]
+                out=squares[:], in_=x_mid[i][:], func=ACT.Square, bias=neg_mean[:, i : i + 1],
+                accum_out=sum_sq[:, i : i + 1],
             )
-            var_eps = stats.tile([P, 1], F32, name="var_eps")
-            nc.gpsimd.tensor_scalar(
-                out=var_eps[:], in0=sum_sq[:], scalar1=1.0 / WIDTH, scalar2=EPS, op0=ALU.mult, op1=ALU.add
-            )
-            rstd[i] = stats.tile([P, 1], F32, name="rstd")
-            nc.gpsimd.tensor_tensor(out=rstd[i][:], in0=var_eps[:], in1=neg_half[:], op=ALU.pow)
+
+        for i in range(TOKEN_TILES):
+            project(i)
+            if i % 2 == 0 and i + 2 < TOKEN_TILES:
+                transpose_attn(i + 2)
+                transpose_attn(i + 3)
+            if i % 2 == 1 and i + 1 < TOKEN_TILES:
+                quantise_attn(i + 1)
+                quantise_attn(i + 2)
+            if i >= TOKEN_TILES - PIECES_PER_CHUNK:
+                prepare_w1(i - (TOKEN_TILES - PIECES_PER_CHUNK))
+        load_w1_chunk(CHUNKS - 1)
+
+        var_eps = keep.tile([P, TOKEN_TILES], F32, name="var_eps")
+        nc.gpsimd.tensor_scalar(out=var_eps[:], in0=sum_sq[:], scalar1=1.0 / WIDTH, scalar2=EPS, op0=ALU.mult, op1=ALU.add)
+        rstd = keep.tile([P, TOKEN_TILES], F32, name="rstd")
+        nc.gpsimd.tensor_tensor(out=rstd[:], in0=var_eps[:], in1=neg_half[:], op=ALU.pow)
+        for k in range(PIECES_PER_CHUNK, PIECES_PER_CHUNK + FILL):
+            prepare_w1(k)
+
+        h2_planes = {}
+        h2_grouped = {}
+        hid_acc = {}
 
         def normalise_and_transpose(i):
+            normed = row("normed")
             nc.vector.tensor_scalar(
-                out=normed[i][:], in0=x_mid[i][:], scalar1=neg_mean[i][:], scalar2=rstd[i][:],
+                out=normed[:], in0=x_mid[i][:], scalar1=neg_mean[:, i : i + 1], scalar2=rstd[:, i : i + 1],
                 op0=ALU.add, op1=ALU.mult,
             )
+            normed_t = [bank("normed_t%d" % c) for c in range(PASSES)]
+            for r in range(K_ROWS):
+                c, t = divmod(r, PACK)
+                nc.tensor.transpose(
+                    out=normed_t[c][:, P * t : P * (t + 1)], in_=normed[:, P * r : P * (r + 1)], identity=identity[:]
+                )
             h2_planes[i] = packs.tile([P, PACK, PASSES * P], BF16, name="h2_planes")
-            for c in range(PASSES):
-                normed_t = bank("normed_t")
-                for t in range(PACK):
-                    r = PACK * c + t
-                    nc.tensor.transpose(
-                        out=normed_t[:, P * t : P * (t + 1)], in_=normed[i][:, P * r : P * (r + 1)], identity=identity[:]
-                    )
-                for t in range(PACK):
-                    r = PACK * c + t
-                    nc.scalar.activation(
-                        out=h2_planes[i][:, t, P * c : P * (c + 1)], in_=normed_t[:, P * t : P * (t + 1)],
-                        func=ACT.Identity, scale=gain_bias[:, r : r + 1], bias=gain_bias[:, K_ROWS + r : K_ROWS + r + 1],
-                    )
+            for r in range(K_ROWS):
+                c, t = divmod(r, PACK)
+                nc.scalar.activation(
+                    out=h2_planes[i][:, t, P * c : P * (c + 1)], in_=normed_t[c][:, P * t : P * (t + 1)],
+                    func=ACT.Identity, scale=gain_bias[:, r : r + 1], bias=gain_bias[:, K_ROWS + r : K_ROWS + r + 1],
+                )
 
         def regroup_h2(i):
             h2_grouped[i] = packs.tile([P, PACK * PASSES * P], BF16, name="h2_grouped", align_bytes=64)
@@ -257,27 +278,34 @@ def tile_transformerblock_pb_kernel(tc, attn, x, w_out, b_out, ln2_g, ln2_b, w1,
         def quantise_h2(i):
             quantise(h2_grouped[i][:], h2_words[:, i, :], h2_scales[:, i, :])
 
-        for s in range(ROUNDS):
-            if s < TOKEN_TILES:
-                project(s)
-            if 1 <= s <= TOKEN_TILES:
-                normalise_and_transpose(s - 1)
-            if s >= 2:
-                regroup_h2(s - 2)
-            prepare_w1(s)
-            if s >= 2:
-                quantise_h2(s - 2)
-            if s == TOKEN_TILES - 1:
-                load_w1_chunk(CHUNKS - 1)
+        def hid_matmul(j, i):
+            hid_acc[(j, i)] = [bank("acc2_%d" % n) for n in range(CHUNK // BANK)]
+            for n in range(CHUNK // BANK):
+                cols = slice(CHUNK * j + BANK * n, CHUNK * j + BANK * (n + 1))
+                multiply(hid_acc[(j, i)][n][:], h2_words, h2_scales, i, w1_words, w1_scales, cols)
 
-        for j in range(CHUNKS):
+        def hid_finish(j, i):
+            hid = row("hid")
+            for n in range(CHUNK // BANK):
+                cols = slice(CHUNK * j + BANK * n, CHUNK * j + BANK * (n + 1))
+                nc.vector.tensor_tensor(
+                    out=hid[:, BANK * n : BANK * (n + 1)], in0=hid_acc[(j, i)][n][:], in1=b1_all[:, cols], op=ALU.add
+                )
+            nc.scalar.activation(out=hid[:], in_=hid[:], func=ACT.Gelu)
+            nc.sync.dma_start(out=hid_rows[:, i, CHUNK * j : CHUNK * (j + 1)], in_=hid[:])
+
+        for r in range(TOKEN_TILES + 3):
+            if r < TOKEN_TILES:
+                normalise_and_transpose(r)
+            if 2 <= r < TOKEN_TILES + 2:
+                regroup_h2(r - 2)
+            prepare_w1(PIECES_PER_CHUNK + FILL + r)
+            if 2 <= r < TOKEN_TILES + 2:
+                quantise_h2(r - 2)
+                hid_matmul(0, r - 2)
+            if r >= 3:
+                hid_finish(0, r - 3)
+        for j in range(1, CHUNKS):
             for i in range(TOKEN_TILES):
-                hid = results.tile([P, CHUNK], F32, name="hid")
-                for n in range(CHUNK // BANK):
-                    cols = slice(CHUNK * j + BANK * n, CHUNK * j + BANK * (n + 1))
-                    acc = bank("acc2")
-                    multiply(acc[:], h2_words, h2_scales, i, w1_words, w1_scales, cols)
-                    nc.vector.tensor_tensor(out=hid[:, BANK * n : BANK * (n + 1)], in0=acc[:], in1=b1_all[:, cols], op=ALU.add)
-                prepare_w1(ROUNDS + TOKEN_TILES * j + i)
-                nc.scalar.activation(out=hid[:], in_=hid[:], func=ACT.Gelu)
-                nc.sync.dma_start(out=hid_rows[:, i, CHUNK * j : CHUNK * (j + 1)], in_=hid[:])
+                hid_matmul(j, i)
+                hid_finish(j, i)

@@ -63,8 +63,9 @@ def tile_transformerblock_pb_kernel(tc, attn, x, w_out, b_out, ln2_g, ln2_b, w1,
         def bank(name):
             return psum.tile([P, BANK], F32, name=name, tag="bank")
 
-        b_out_all = keep.tile([P, WIDTH], BF16, name="b_out_all")
-        nc.sync.dma_start(out=b_out_all[:], in_=b_out.partition_broadcast(P))
+        b_out_row = keep.tile([P, WIDTH], BF16, name="b_out_row")
+        nc.vector.memset(b_out_row[:], 0.0)
+        nc.sync.dma_start(out=b_out_row[0:1, :], in_=b_out.rearrange("(o d) -> o d", o=1))
         gain_bias_rows = keep.tile([P, P], BF16, name="gain_bias_rows")
         nc.vector.memset(gain_bias_rows[:], 0.0)
         nc.sync.dma_start(out=gain_bias_rows[0:K_ROWS, :], in_=ln2_g.rearrange("(r p) -> r p", p=P))
@@ -100,6 +101,15 @@ def tile_transformerblock_pb_kernel(tc, attn, x, w_out, b_out, ln2_g, ln2_b, w1,
         nc.scalar.activation(out=table_warm[:], in_=neg_half[:, 0:1], func=ACT.Gelu)
         identity = keep.tile([P, P], F32, name="identity")
         masks.make_identity(nc, identity[:])
+
+        ones = keep.tile([P, P], BF16, name="ones")
+        nc.vector.memset(ones[:], 1.0)
+        b_out_all = keep.tile([P, WIDTH], BF16, name="b_out_all")
+        for n in range(WIDTH // BANK):
+            cols = slice(BANK * n, BANK * (n + 1))
+            spread = bank("spread")
+            nc.tensor.matmul(out=spread[:], lhsT=ones[:], rhs=b_out_row[:, cols], start=True, stop=True)
+            nc.scalar.copy(out=b_out_all[:, cols], in_=spread[:])
 
         def quantised(name, outer, width):
             words = keep.tile([P, outer, width], U32, name=name + "_words", align_bytes=64)
@@ -284,15 +294,20 @@ def tile_transformerblock_pb_kernel(tc, attn, x, w_out, b_out, ln2_g, ln2_b, w1,
                 cols = slice(CHUNK * j + BANK * n, CHUNK * j + BANK * (n + 1))
                 multiply(hid_acc[(j, i)][n][:], h2_words, h2_scales, i, w1_words, w1_scales, cols)
 
-        def hid_finish(j, i):
+        def hid_finish(j, i, banks_at_a_time):
             hid = row("hid")
-            for n in range(CHUNK // BANK):
-                cols = slice(CHUNK * j + BANK * n, CHUNK * j + BANK * (n + 1))
-                nc.vector.tensor_tensor(
-                    out=hid[:, BANK * n : BANK * (n + 1)], in0=hid_acc[(j, i)][n][:], in1=b1_all[:, cols], op=ALU.add
+            for first in range(0, CHUNK // BANK, banks_at_a_time):
+                for n in range(first, first + banks_at_a_time):
+                    nc.vector.tensor_tensor(
+                        out=hid[:, BANK * n : BANK * (n + 1)], in0=hid_acc[(j, i)][n][:],
+                        in1=b1_all[:, CHUNK * j + BANK * n : CHUNK * j + BANK * (n + 1)], op=ALU.add,
+                    )
+                part = slice(BANK * first, BANK * (first + banks_at_a_time))
+                nc.scalar.activation(out=hid[:, part], in_=hid[:, part], func=ACT.Gelu)
+                nc.sync.dma_start(
+                    out=hid_rows[:, i, CHUNK * j + BANK * first : CHUNK * j + BANK * (first + banks_at_a_time)],
+                    in_=hid[:, part],
                 )
-            nc.scalar.activation(out=hid[:], in_=hid[:], func=ACT.Gelu)
-            nc.sync.dma_start(out=hid_rows[:, i, CHUNK * j : CHUNK * (j + 1)], in_=hid[:])
 
         for r in range(TOKEN_TILES + 3):
             if r < TOKEN_TILES:
@@ -304,8 +319,9 @@ def tile_transformerblock_pb_kernel(tc, attn, x, w_out, b_out, ln2_g, ln2_b, w1,
                 quantise_h2(r - 2)
                 hid_matmul(0, r - 2)
             if r >= 3:
-                hid_finish(0, r - 3)
+                hid_finish(0, r - 3, CHUNK // BANK)
         for j in range(1, CHUNKS):
             for i in range(TOKEN_TILES):
+                last = j == CHUNKS - 1 and i == TOKEN_TILES - 1
                 hid_matmul(j, i)
-                hid_finish(j, i)
+                hid_finish(j, i, 1 if last else CHUNK // BANK)

from contextlib import ExitStack

import concourse.masks as masks
import concourse.mybir as mybir

F32 = mybir.dt.float32
BF16 = mybir.dt.bfloat16
U32 = mybir.dt.uint32
U8 = mybir.dt.uint8
FP8X4 = mybir.dt.float8_e4m3fn_x4
ALU = mybir.AluOpType
ACT = mybir.ActivationFunctionType

P = 128
PACK = 4
K_PASS = P * PACK
BANK = 512
RUN = 4

TOKENS = 1024
WIDTH = 1024
HIDDEN = 4096
EPS = 1e-5
TOKEN_TILES = TOKENS // P
K_ROWS = WIDTH // P
PASSES = WIDTH // K_PASS
CHUNK = 1024
CHUNKS = HIDDEN // CHUNK
PIECE = BANK
PIECES_PER_CHUNK = PASSES * (CHUNK // PIECE)
W1_PIECES = CHUNKS * PIECES_PER_CHUNK
VECTOR_EVERY = 4
FILL = 2
FIRST_TILES = 2

FLOPS = 2 * TOKENS * WIDTH * WIDTH + 2 * TOKENS * WIDTH * HIDDEN


def regroup(copy, grouped, rows):
    copy(
        out=grouped.rearrange("p (a i t) -> p a t i", i=RUN, t=PACK),
        in_=rows.rearrange("p t (a i) -> p a t i", i=RUN),
    )


def tile_transformerblock_pb_kernel(tc, attn, x, w_out, b_out, ln2_g, ln2_b, w1, b1, out_0, out_1):
    nc = tc.nc
    attn_rows = attn.flatten_outer_dims().rearrange("(p i) k -> p i k", i=TOKEN_TILES)
    x_rows = x.flatten_outer_dims().rearrange("(p i) d -> p i d", i=TOKEN_TILES)
    x_mid_rows = out_0.flatten_outer_dims().rearrange("(p i) d -> p i d", i=TOKEN_TILES)
    hid_rows = out_1.flatten_outer_dims().rearrange("(p i) f -> p i f", i=TOKEN_TILES)
    w_out_rows = w_out.rearrange("(g u q e) n -> g q u e n", g=PASSES, u=2, q=P, e=2)
    w1_rows = w1.rearrange("(c t p) f -> p (c t) f", c=PASSES, t=PACK, p=P)

    with ExitStack() as ctx:
        keep = ctx.enter_context(tc.tile_pool(name="keep", bufs=1))
        raw = ctx.enter_context(tc.tile_pool(name="raw", bufs=3))
        pieces = ctx.enter_context(tc.tile_pool(name="pieces", bufs=3))
        packs = ctx.enter_context(tc.tile_pool(name="packs", bufs=2))
        rows = ctx.enter_context(tc.tile_pool(name="rows", bufs=14))
        psum = ctx.enter_context(tc.psum_pool(name="psum", bufs=8))

        def bank(name):
            return psum.tile([P, BANK], F32, name=name, tag="bank")

        b_out_row = keep.tile([P, WIDTH], BF16, name="b_out_row")
        nc.vector.memset(b_out_row[:], 0.0)
        nc.sync.dma_start(out=b_out_row[0:1, :], in_=b_out.rearrange("(o d) -> o d", o=1))
        gain_bias_rows = keep.tile([P, P], BF16, name="gain_bias_rows")
        nc.vector.memset(gain_bias_rows[:], 0.0)
        nc.sync.dma_start(out=gain_bias_rows[0:K_ROWS, :], in_=ln2_g.rearrange("(r p) -> r p", p=P))
        nc.sync.dma_start(out=gain_bias_rows[K_ROWS : 2 * K_ROWS, :], in_=ln2_b.rearrange("(r p) -> r p", p=P))

        def raw_tile(name):
            return raw.tile([P, PASSES * PACK, CHUNK], BF16, name=name, tag="raw")

        def load_w1_chunk(j):
            w1_raw[j] = raw_tile("w1_raw%d" % j)
            nc.sync.dma_start(out=w1_raw[j][:], in_=w1_rows[:, :, CHUNK * j : CHUNK * (j + 1)])

        w_out_raw = raw_tile("w_out_raw")
        for g in range(PASSES):
            nc.sync.dma_start(
                out=w_out_raw[:, PACK * g : PACK * (g + 1), :].rearrange("q (u e) n -> q u e n", u=2),
                in_=w_out_rows[g],
            )
        attn_raw = raw_tile("attn_raw")
        x_raw = keep.tile([P, TOKEN_TILES, WIDTH], BF16, name="x_raw")
        for tiles in (slice(0, FIRST_TILES), slice(FIRST_TILES, TOKEN_TILES)):
            nc.sync.dma_start(out=attn_raw[:, tiles, :], in_=attn_rows[:, tiles, :])
            nc.sync.dma_start(out=x_raw[:, tiles, :], in_=x_rows[:, tiles, :])
        w1_raw = {}
        for j in range(CHUNKS - 1):
            load_w1_chunk(j)
        b1_all = keep.tile([P, HIDDEN], BF16, name="b1_all")
        nc.sync.dma_start(out=b1_all[:], in_=b1.partition_broadcast(P))

        neg_half = keep.tile([P, TOKEN_TILES], F32, name="neg_half")
        nc.vector.memset(neg_half[:], -0.5)
        table_warm = keep.tile([P, 1], F32, name="table_warm")
        nc.scalar.activation(out=table_warm[:], in_=neg_half[:, 0:1], func=ACT.Gelu)
        identity = keep.tile([P, P], F32, name="identity")
        masks.make_identity(nc, identity[:])

        ones = keep.tile([P, P], BF16, name="ones")
        nc.vector.memset(ones[:], 1.0)
        b_out_all = keep.tile([P, WIDTH], BF16, name="b_out_all")
        for n in range(WIDTH // BANK):
            cols = slice(BANK * n, BANK * (n + 1))
            spread = bank("spread")
            nc.tensor.matmul(out=spread[:], lhsT=ones[:], rhs=b_out_row[:, cols], start=True, stop=True)
            nc.scalar.copy(out=b_out_all[:, cols], in_=spread[:])

        def quantised(name, outer, width):
            words = keep.tile([P, outer, width], U32, name=name + "_words", align_bytes=64)
            scales = keep.tile([P, outer, width], U8, name=name + "_scales", align_bytes=64)
            return words, scales

        w_out_words, w_out_scales = quantised("w_out", PASSES, WIDTH)
        w1_words, w1_scales = quantised("w1", PASSES, HIDDEN)
        attn_words, attn_scales = quantised("attn", TOKEN_TILES, PASSES * P)
        h2_words, h2_scales = quantised("h2", TOKEN_TILES, PASSES * P)

        def quantise(grouped, words, scales):
            nc.vector.quantize_mx(out=words.bitcast(FP8X4), scales=scales, in_=grouped)

        def multiply(acc, lhs_words, lhs_scales, i, rhs_words, rhs_scales, cols):
            for c in range(PASSES):
                tokens = slice(P * c, P * (c + 1))
                nc.tensor.matmul_mx(
                    out=acc,
                    lhsT=lhs_words[:, i, tokens].bitcast(FP8X4),
                    lhsT_scale=lhs_scales[:, i, tokens],
                    rhs=rhs_words[:, c, cols].bitcast(FP8X4),
                    rhs_scale=rhs_scales[:, c, cols],
                    start=(c == 0),
                    stop=(c == PASSES - 1),
                )

        piece_tiles = {}

        def regroup_piece(key, copy, raw_rows):
            piece_tiles[key] = pieces.tile([P, PACK * PIECE], BF16, name="piece", tag="piece", align_bytes=64)
            regroup(copy, piece_tiles[key][:], raw_rows)

        def w1_piece(k):
            j, rest = divmod(k, PIECES_PER_CHUNK)
            c, n = divmod(rest, CHUNK // PIECE)
            return j, c, slice(CHUNK * j + PIECE * n, CHUNK * j + PIECE * (n + 1)), slice(PIECE * n, PIECE * (n + 1))

        def regroup_w1_piece(k, copy):
            j, c, cols, cols_in_chunk = w1_piece(k)
            regroup_piece(("w1", k), copy, w1_raw[j][:, PACK * c : PACK * (c + 1), cols_in_chunk])

        def quantise_w1_piece(k):
            j, c, cols, cols_in_chunk = w1_piece(k)
            quantise(piece_tiles[("w1", k)][:], w1_words[:, c, cols], w1_scales[:, c, cols])

        def prepare_w1(k):
            if k < W1_PIECES:
                regroup_w1_piece(k, nc.vector.tensor_copy if k % VECTOR_EVERY == 0 else nc.scalar.copy)
            if 1 <= k <= W1_PIECES:
                quantise_w1_piece(k - 1)

        w_out_pieces = [(g, slice(PIECE * n, PIECE * (n + 1))) for g in range(PASSES) for n in range(WIDTH // PIECE)]
        for k in range(len(w_out_pieces) + 1):
            if k < len(w_out_pieces):
                g, cols = w_out_pieces[k]
                copy = nc.vector.tensor_copy if k % 2 == 0 else nc.scalar.copy
                regroup_piece(("w_out", k), copy, w_out_raw[:, PACK * g : PACK * (g + 1), cols])
            if k > 0:
                g, cols = w_out_pieces[k - 1]
                quantise(piece_tiles[("w_out", k - 1)][:], w_out_words[:, g, cols], w_out_scales[:, g, cols])

        attn_grouped = {}

        def transpose_attn(i):
            attn_pairs = attn_raw[:, i, :].bitcast(F32)
            attn_t = bank("attn_t")
            for g in range(PASSES):
                for u in range(2):
                    block = 2 * g + u
                    nc.tensor.transpose(
                        out=attn_t[:, PASSES * P * u + P * g : PASSES * P * u + P * (g + 1)],
                        in_=attn_pairs[:, P * block : P * (block + 1)],
                        identity=identity[:],
                    )
            attn_grouped[i] = packs.tile([P, PACK * PASSES * P], BF16, name="attn_grouped", align_bytes=64)
            nc.scalar.copy(
                out=attn_grouped[i][:].bitcast(F32).rearrange("q (m u) -> q m u", u=2),
                in_=attn_t[:].rearrange("q (u m) -> q m u", u=2),
            )

        def quantise_attn(i):
            quantise(attn_grouped[i][:], attn_words[:, i, :], attn_scales[:, i, :])

        for i in range(FIRST_TILES):
            transpose_attn(i)
        for i in range(FIRST_TILES):
            quantise_attn(i)

        gain_bias_f32 = keep.tile([P, P], F32, name="gain_bias_f32")
        nc.vector.tensor_copy(out=gain_bias_f32[:], in_=gain_bias_rows[:])
        gain_bias_t = bank("gain_bias_t")
        nc.tensor.transpose(out=gain_bias_t[:, 0:P], in_=gain_bias_f32[:], identity=identity[:])
        gain_bias = keep.tile([P, 2 * K_ROWS], F32, name="gain_bias")
        nc.vector.tensor_copy(out=gain_bias[:], in_=gain_bias_t[:, 0 : 2 * K_ROWS])

        def row(name):
            return rows.tile([P, WIDTH], F32, name=name, tag="row")

        x_mid = {}
        row_sums = keep.tile([P, TOKEN_TILES, WIDTH // BANK], F32, name="row_sums")
        scaled_sums = keep.tile([P, WIDTH // BANK], F32, name="scaled_sums")
        neg_mean = keep.tile([P, TOKEN_TILES], F32, name="neg_mean")
        squares = keep.tile([P, WIDTH], BF16, name="squares")
        sum_sq = keep.tile([P, TOKEN_TILES], F32, name="sum_sq")

        def project(i):
            x_bias = row("x_bias")
            nc.vector.tensor_tensor(out=x_bias[:], in0=x_raw[:, i, :], in1=b_out_all[:], op=ALU.add)
            x_mid[i] = row("x_mid")
            for n in range(WIDTH // BANK):
                cols = slice(BANK * n, BANK * (n + 1))
                acc = bank("acc1")
                multiply(acc[:], attn_words, attn_scales, i, w_out_words, w_out_scales, cols)
                nc.vector.scalar_tensor_tensor(
                    out=x_mid[i][:, cols], in0=acc[:], scalar=1.0, in1=x_bias[:, cols],
                    op0=ALU.mult, op1=ALU.add, accum_out=row_sums[:, i, n : n + 1],
                )
            nc.sync.dma_start(out=x_mid_rows[:, i, :], in_=x_mid[i][:])
            nc.scalar.activation(
                out=scaled_sums[:], in_=row_sums[:, i, :], func=ACT.Identity, scale=-1.0 / WIDTH,
                accum_out=neg_mean[:, i : i + 1],
            )
            nc.scalar.activation(
                out=squares[:], in_=x_mid[i][:], func=ACT.Square, bias=neg_mean[:, i : i + 1],
                accum_out=sum_sq[:, i : i + 1],
            )

        for i in range(TOKEN_TILES):
            project(i)
            if i % 2 == 0 and i + 2 < TOKEN_TILES:
                transpose_attn(i + 2)
                transpose_attn(i + 3)
            if i % 2 == 1 and i + 1 < TOKEN_TILES:
                quantise_attn(i + 1)
                quantise_attn(i + 2)
            if i >= TOKEN_TILES - PIECES_PER_CHUNK:
                prepare_w1(i - (TOKEN_TILES - PIECES_PER_CHUNK))
        load_w1_chunk(CHUNKS - 1)

        var_eps = keep.tile([P, TOKEN_TILES], F32, name="var_eps")
        nc.gpsimd.tensor_scalar(out=var_eps[:], in0=sum_sq[:], scalar1=1.0 / WIDTH, scalar2=EPS, op0=ALU.mult, op1=ALU.add)
        rstd = keep.tile([P, TOKEN_TILES], F32, name="rstd")
        nc.gpsimd.tensor_tensor(out=rstd[:], in0=var_eps[:], in1=neg_half[:], op=ALU.pow)
        for k in range(PIECES_PER_CHUNK, PIECES_PER_CHUNK + FILL):
            prepare_w1(k)

        h2_planes = {}
        h2_grouped = {}
        hid_acc = {}

        def normalise_and_transpose(i):
            normed = row("normed")
            nc.vector.tensor_scalar(
                out=normed[:], in0=x_mid[i][:], scalar1=neg_mean[:, i : i + 1], scalar2=rstd[:, i : i + 1],
                op0=ALU.add, op1=ALU.mult,
            )
            normed_t = [bank("normed_t%d" % c) for c in range(PASSES)]
            for r in range(K_ROWS):
                c, t = divmod(r, PACK)
                nc.tensor.transpose(
                    out=normed_t[c][:, P * t : P * (t + 1)], in_=normed[:, P * r : P * (r + 1)], identity=identity[:]
                )
            h2_planes[i] = packs.tile([P, PACK, PASSES * P], BF16, name="h2_planes")
            for r in range(K_ROWS):
                c, t = divmod(r, PACK)
                nc.scalar.activation(
                    out=h2_planes[i][:, t, P * c : P * (c + 1)], in_=normed_t[c][:, P * t : P * (t + 1)],
                    func=ACT.Identity, scale=gain_bias[:, r : r + 1], bias=gain_bias[:, K_ROWS + r : K_ROWS + r + 1],
                )

        def regroup_h2(i):
            h2_grouped[i] = packs.tile([P, PACK * PASSES * P], BF16, name="h2_grouped", align_bytes=64)
            regroup(nc.vector.tensor_copy, h2_grouped[i][:], h2_planes[i][:])

        def quantise_h2(i):
            quantise(h2_grouped[i][:], h2_words[:, i, :], h2_scales[:, i, :])

        def hid_matmul(j, i):
            hid_acc[(j, i)] = [bank("acc2_%d" % n) for n in range(CHUNK // BANK)]
            for n in range(CHUNK // BANK):
                cols = slice(CHUNK * j + BANK * n, CHUNK * j + BANK * (n + 1))
                multiply(hid_acc[(j, i)][n][:], h2_words, h2_scales, i, w1_words, w1_scales, cols)

        def hid_finish(j, i, banks_at_a_time):
            hid = row("hid")
            for first in range(0, CHUNK // BANK, banks_at_a_time):
                for n in range(first, first + banks_at_a_time):
                    nc.vector.tensor_tensor(
                        out=hid[:, BANK * n : BANK * (n + 1)], in0=hid_acc[(j, i)][n][:],
                        in1=b1_all[:, CHUNK * j + BANK * n : CHUNK * j + BANK * (n + 1)], op=ALU.add,
                    )
                part = slice(BANK * first, BANK * (first + banks_at_a_time))
                nc.scalar.activation(out=hid[:, part], in_=hid[:, part], func=ACT.Gelu)
                nc.sync.dma_start(
                    out=hid_rows[:, i, CHUNK * j + BANK * first : CHUNK * j + BANK * (first + banks_at_a_time)],
                    in_=hid[:, part],
                )

        for r in range(TOKEN_TILES + 3):
            if r < TOKEN_TILES:
                normalise_and_transpose(r)
            if 2 <= r < TOKEN_TILES + 2:
                regroup_h2(r - 2)
            prepare_w1(PIECES_PER_CHUNK + FILL + r)
            if 2 <= r < TOKEN_TILES + 2:
                quantise_h2(r - 2)
                hid_matmul(0, r - 2)
            if r >= 3:
                hid_finish(0, r - 3, CHUNK // BANK)
        for j in range(1, CHUNKS):
            for i in range(TOKEN_TILES):
                last = j == CHUNKS - 1 and i == TOKEN_TILES - 1
                hid_matmul(j, i)
                hid_finish(j, i, 1 if last else CHUNK // BANK)
